import numpy as np
import ml_dtypes


def mxq(x, axis, fmt="e4m3"):
    dtype, down = {"e4m3": (ml_dtypes.float8_e4m3fn, 7), "e5m2": (ml_dtypes.float8_e5m2, 14)}[fmt]
    v = np.moveaxis(np.asarray(x, np.float32).astype(ml_dtypes.bfloat16).astype(np.float64), axis, -1)
    blocks = v.reshape(v.shape[:-1] + (-1, 32))
    amax = np.abs(blocks).max(-1, keepdims=True)
    byte = np.maximum(np.where(amax > 0, np.frexp(amax)[1] - 1 + 127, 0) - down, 1)
    scale = np.exp2(byte - 127.0)
    codes = (blocks / scale).astype(np.float32).astype(dtype).astype(np.float64)
    return np.moveaxis((codes * scale).reshape(v.shape), -1, axis)


WIDE = False


def mx_kscale(k):
    if not WIDE:
        return np.ones(k)
    levels = np.array([10, -10, 5, -5, 0])
    a = np.random.permutation(np.resize(levels, k // 512 * 4)).reshape(k // 512, 4)
    idx = np.arange(k)
    return np.exp2(a[idx // 512, idx % 128 // 32])


BF16 = ml_dtypes.bfloat16


def bf(x):
    return np.asarray(x, np.float32).astype(BF16)


def f64(x):
    return np.asarray(x).astype(np.float64)


S, H, E, P, C = 1024, 256, 416, 64, 32
IN0 = E + P + C + 4 * H


def sigmoid(v):
    return 1.0 / (1.0 + np.exp(-v))


def lstm_gates(g, c):
    i, f, gg, o = np.split(g, 4, axis=-1)
    c2 = sigmoid(f) * c + sigmoid(i) * np.tanh(gg)
    return sigmoid(o) * np.tanh(c2)


def setup_inputs():
    n = np.random.standard_normal
    s = mx_kscale(IN0)
    a1, a2, a3, a4 = 2 * H, 4 * H, 4 * H + E, 4 * H + E + P
    d = {"hn_chunks": bf(n((S, 2 * H)) * s[:a1]), "hn_tags": bf(n((S, 2 * H)) * s[a1:a2]), "x": bf(n((S, E)) * s[a2:a3]),
         "tags": bf(n((S, P)) * s[a3:a4]), "chunks": bf(n((S, C)) * s[a4:]),
         "h0": bf(n((2, S, H))), "c0": bf(n((2, S, H)))}
    for k in ("f", "b"):
        d["wih_" + k] = bf(n((4 * H, IN0)) / np.sqrt(IN0) / s)
        d["whh_" + k] = bf(n((4 * H, H)) * 0.7 / np.sqrt(H))
        d["bih_" + k] = bf(n(4 * H) * 0.2)
        d["bhh_" + k] = bf(n(4 * H) * 0.2)
    return d


def reference(hn_chunks, hn_tags, x, tags, chunks, h0, c0, wih_f, whh_f, bih_f, bhh_f, wih_b, whh_b, bih_b, bhh_b):
    gt = np.concatenate([f64(hn_chunks), f64(hn_tags), f64(x), f64(tags), f64(chunks)], axis=1)
    gq = mxq(gt, 1, "e4m3")
    gf = (gq @ mxq(f64(wih_f), 1, "e4m3").T) + f64(bih_f) + f64(h0)[0] @ f64(whh_f).T + f64(bhh_f)
    gb = (gq @ mxq(f64(wih_b), 1, "e4m3").T) + f64(bih_b) + f64(h0)[1] @ f64(whh_b).T + f64(bhh_b)
    return np.concatenate([lstm_gates(gf, f64(c0)[0]), lstm_gates(gb, f64(c0)[1])], axis=-1)

@@ -1,0 +1,198 @@
+from contextlib import ExitStack
+
+import concourse.mybir as mybir
+from concourse.masks import make_identity
+
+F32 = mybir.dt.float32
+BF16 = mybir.dt.bfloat16
+U32 = mybir.dt.uint32
+U8 = mybir.dt.uint8
+FP8X4 = mybir.dt.float8_e4m3fn_x4
+ACT = mybir.ActivationFunctionType
+ALU = mybir.AluOpType
+
+P = 128
+TOKENS = 1024
+TOKEN_TILES = TOKENS // P
+HID = 256
+GATES = 4 * HID
+K_IN = 1536
+K_PASS = 512
+PASSES = K_IN // K_PASS
+WORDS = K_PASS // 2
+BANK = 512
+BANKS = GATES // BANK
+ROW_TILES = 2
+STEP_COLS = ROW_TILES * P
+
+FLOPS = 2 * TOKENS * (K_IN + HID) * 2 * GATES
+
+
+def tile_dependency_pa_kernel(
+    tc, hn_chunks, hn_tags, x, tags, chunks, h0, c0,
+    wih_f, whh_f, bih_f, bhh_f, wih_b, whh_b, bih_b, bhh_b, out,
+):
+    nc = tc.nc
+    wih = (wih_f, wih_b)
+    whh = (whh_f, whh_b)
+    bih = (bih_f, bih_b)
+    bhh = (bhh_f, bhh_b)
+
+    with ExitStack() as ctx:
+        consts = ctx.enter_context(tc.tile_pool(name="consts", bufs=1))
+        keep = ctx.enter_context(tc.tile_pool(name="keep", bufs=1))
+        wih_pool = ctx.enter_context(tc.tile_pool(name="wih_pool", bufs=4))
+        stage = ctx.enter_context(tc.tile_pool(name="stage", bufs=4))
+        flip_psum = ctx.enter_context(tc.psum_pool(name="flip_psum", bufs=3))
+        sum_psum = ctx.enter_context(tc.psum_pool(name="sum_psum", bufs=5))
+
+        ident_bf = consts.tile([P, P], BF16)
+        make_identity(nc, ident_bf[:])
+        ident_f32 = consts.tile([P, P], F32)
+        make_identity(nc, ident_f32[:])
+        ones = consts.tile([P, P], BF16)
+        nc.vector.memset(ones[:], 1.0)
+        warm = consts.tile([P, 1], F32)
+        nc.vector.memset(warm[:], 0.0)
+        nc.scalar.activation(out=warm[:], in_=warm[:], func=ACT.Sigmoid)
+
+        h0T = [keep.tile([P, HID // P, TOKENS], BF16, name="h0T%d" % d) for d in range(2)]
+        whhT = [keep.tile([P, HID // P, GATES], BF16, name="whhT%d" % d) for d in range(2)]
+        c0_sb = [keep.tile([P, TOKEN_TILES, HID], BF16, name="c0_sb%d" % d) for d in range(2)]
+        gt_raw = [keep.tile([P, TOKEN_TILES * K_PASS], BF16, name="gt_raw%d" % g) for g in range(PASSES)]
+        gt_codes = keep.tile([P, PASSES, TOKENS], U32, align_bytes=64)
+        gt_scales = keep.tile([P, PASSES, TOKENS], U8, align_bytes=64)
+        w_codes = [keep.tile([P, PASSES, GATES], U32, align_bytes=64, name="w_codes%d" % d) for d in range(2)]
+        w_scales = [keep.tile([P, PASSES, GATES], U8, align_bytes=64, name="w_scales%d" % d) for d in range(2)]
+        gates = [keep.tile([P, TOKEN_TILES, GATES], F32, name="gates%d" % d) for d in range(2)]
+        bias_rows = consts.tile([P, 2 * GATES], BF16)
+        bias_all = consts.tile([P, 2 * GATES], F32)
+
+        def quantise_step(rows, codes, scales):
+            flipped = flip_psum.tile([P, ROW_TILES, 2, P], F32, tag="flipped")
+            for r in range(ROW_TILES):
+                for u in range(2):
+                    nc.tensor.transpose(out=flipped[:, r, u, :], in_=rows[r][:, u * P:(u + 1) * P], identity=ident_f32[:])
+            grouped = stage.tile([P, 4 * STEP_COLS], BF16, align_bytes=64)
+            nc.scalar.copy(
+                out=grouped[:].bitcast(F32).rearrange("p (r c u) -> p r c u", r=ROW_TILES, u=2),
+                in_=flipped[:].rearrange("p r u c -> p r c u"),
+            )
+            nc.vector.quantize_mx(out=codes.bitcast(FP8X4), scales=scales, in_=grouped[:])
+
+        def transpose_hidden(raw, flat):
+            for kt in range(HID // P):
+                for half in range(2):
+                    flipped = flip_psum.tile([P, 4, P], BF16, tag="flipped")
+                    for i in range(4):
+                        first = (4 * half + i) * HID + kt * P
+                        nc.tensor.transpose(out=flipped[:, i, :], in_=raw[:, first:first + P], identity=ident_bf[:])
+                    nc.scalar.copy(out=flat[:, kt, 4 * half * P:4 * (half + 1) * P], in_=flipped[:].rearrange("p i r -> p (i r)"))
+
+        def hidden_product(d):
+            for t in range(TOKEN_TILES):
+                for b in range(BANKS):
+                    cols = slice(b * BANK, (b + 1) * BANK)
+                    acc = sum_psum.tile([P, BANK], F32, tag="acc")
+                    for kt in range(HID // P):
+                        nc.tensor.matmul(
+                            out=acc[:], lhsT=h0T[d][:, kt, t * P:(t + 1) * P], rhs=whhT[d][:, kt, cols],
+                            start=(kt == 0), stop=(kt == HID // P - 1),
+                        )
+                    nc.vector.tensor_tensor(
+                        out=gates[d][:, t, cols], in0=acc[:],
+                        in1=bias_all[:, d * GATES + b * BANK:d * GATES + (b + 1) * BANK], op=ALU.add,
+                    )
+
+        def quantise_weights(d):
+            chunks_of_rows = wih[d].rearrange("(c r p) k -> c p r k", r=ROW_TILES, p=P)
+            for c in range(GATES // STEP_COLS):
+                w_raw = wih_pool.tile([P, ROW_TILES * K_IN], BF16)
+                nc.sync.dma_start(out=w_raw[:].rearrange("p (r k) -> p r k", r=ROW_TILES), in_=chunks_of_rows[c])
+                words = w_raw[:].bitcast(F32)
+                for g in range(PASSES):
+                    firsts = [r * (K_IN // 2) + g * WORDS for r in range(ROW_TILES)]
+                    cols = slice(c * STEP_COLS, (c + 1) * STEP_COLS)
+                    quantise_step([words[:, f:f + WORDS] for f in firsts], w_codes[d][:, g, cols], w_scales[d][:, g, cols])
+
+        def lstm_direction(d):
+            out_view = out.rearrange("(p t) c -> p t c", t=TOKEN_TILES)
+            for pair in range(TOKEN_TILES // 2):
+                two = slice(2 * pair, 2 * pair + 2)
+                for b in range(BANKS):
+                    cols = slice(b * BANK, (b + 1) * BANK)
+                    for t in range(2 * pair, 2 * pair + 2):
+                        acc = sum_psum.tile([P, BANK], F32, tag="acc")
+                        for g in range(PASSES):
+                            nc.tensor.matmul_mx(
+                                out=acc[:],
+                                lhsT=gt_codes[:, g, t * P:(t + 1) * P].bitcast(FP8X4),
+                                lhsT_scale=gt_scales[:, g, t * P:(t + 1) * P],
+                                rhs=w_codes[d][:, g, cols].bitcast(FP8X4),
+                                rhs_scale=w_scales[d][:, g, cols],
+                                start=(g == 0), stop=(g == PASSES - 1),
+                            )
+                        nc.vector.tensor_tensor(out=gates[d][:, t, cols], in0=acc[:], in1=gates[d][:, t, cols], op=ALU.add)
+                gate_i = gates[d][:, two, 0:HID]
+                gate_f = gates[d][:, two, HID:2 * HID]
+                gate_g = gates[d][:, two, 2 * HID:3 * HID]
+                gate_o = gates[d][:, two, 3 * HID:4 * HID]
+                nc.scalar.activation(out=gates[d][:, two, 0:2 * HID], in_=gates[d][:, two, 0:2 * HID], func=ACT.Sigmoid)
+                nc.scalar.activation(out=gate_g, in_=gate_g, func=ACT.Tanh)
+                nc.scalar.activation(out=gate_o, in_=gate_o, func=ACT.Sigmoid)
+                kept = cell_pool.tile([P, 2, HID], F32)
+                nc.vector.tensor_tensor(out=kept[:], in0=gate_f, in1=c0_sb[d][:, two, :], op=ALU.mult)
+                fresh = cell_pool.tile([P, 2, HID], F32)
+                nc.vector.tensor_tensor(out=fresh[:], in0=gate_i, in1=gate_g, op=ALU.mult)
+                cell = cell_pool.tile([P, 2, HID], F32)
+                nc.vector.tensor_tensor(out=cell[:], in0=kept[:], in1=fresh[:], op=ALU.add)
+                nc.scalar.activation(out=cell[:], in_=cell[:], func=ACT.Tanh)
+                hidden = cell_pool.tile([P, 2, HID], F32)
+                nc.vector.tensor_tensor(out=hidden[:], in0=gate_o, in1=cell[:], op=ALU.mult)
+                nc.sync.dma_start(out=out_view[:, two, d * HID:(d + 1) * HID], in_=hidden[:])
+
+        with tc.tile_pool(name="hidden_raw", bufs=1) as hidden_raw:
+            h0_raw = [hidden_raw.tile([P, TOKEN_TILES * HID], BF16, name="h0_raw%d" % d) for d in range(2)]
+            whh_raw = [hidden_raw.tile([P, TOKEN_TILES * HID], BF16, name="whh_raw%d" % d) for d in range(2)]
+            nc.vector.memset(bias_rows[:], 0.0)
+            for d in range(2):
+                nc.scalar.dma_start(out=bias_rows[0:1, d * GATES:(d + 1) * GATES], in_=bih[d].rearrange("(o n) -> o n", o=1))
+                nc.scalar.dma_start(out=bias_rows[1:2, d * GATES:(d + 1) * GATES], in_=bhh[d].rearrange("(o n) -> o n", o=1))
+            for d in range(2):
+                nc.sync.dma_start(out=h0_raw[d][:], in_=h0[d].rearrange("(p t) k -> p (t k)", t=TOKEN_TILES))
+                nc.sync.dma_start(
+                    out=whh_raw[d][:].rearrange("p (t k) -> p t k", t=TOKEN_TILES),
+                    in_=whh[d].rearrange("(t p) k -> p t k", p=P),
+                )
+            nc.sync.dma_start(out=gt_raw[0][:], in_=hn_chunks.rearrange("(p t) k -> p (t k)", t=TOKEN_TILES))
+            nc.sync.dma_start(out=gt_raw[1][:], in_=hn_tags.rearrange("(p t) k -> p (t k)", t=TOKEN_TILES))
+            last_pass = gt_raw[2][:].rearrange("p (t k) -> p t k", t=TOKEN_TILES)
+            first = 0
+            for stream in (x, tags, chunks):
+                width = stream.shape[1]
+                nc.sync.dma_start(out=last_pass[:, :, first:first + width], in_=stream.rearrange("(p t) k -> p t k", t=TOKEN_TILES))
+                first += width
+
+            for q in range(2 * BANKS):
+                acc = sum_psum.tile([P, BANK], F32, tag="acc")
+                nc.tensor.matmul(out=acc[:], lhsT=ones[:], rhs=bias_rows[:, q * BANK:(q + 1) * BANK], start=True, stop=True)
+                nc.vector.tensor_copy(out=bias_all[:, q * BANK:(q + 1) * BANK], in_=acc[:])
+            for d in range(2):
+                transpose_hidden(h0_raw[d], h0T[d])
+                transpose_hidden(whh_raw[d], whhT[d])
+
+        cell_pool = ctx.enter_context(tc.tile_pool(name="cell_pool", bufs=2))
+        hidden_product(0)
+        for g in range(PASSES):
+            words = gt_raw[g][:].bitcast(F32)
+            for s in range(TOKENS // STEP_COLS):
+                cols = slice(s * STEP_COLS, (s + 1) * STEP_COLS)
+                firsts = [(ROW_TILES * s + r) * WORDS for r in range(ROW_TILES)]
+                quantise_step([words[:, f:f + WORDS] for f in firsts], gt_codes[:, g, cols], gt_scales[:, g, cols])
+        quantise_weights(0)
+        for d in range(2):
+            nc.sync.dma_start(out=c0_sb[d][:], in_=c0[d].rearrange("(p t) k -> p t k", t=TOKEN_TILES))
+        hidden_product(1)
+        quantise_weights(1)
+        lstm_direction(0)
+        lstm_direction(1)

@@ -15,6 +15,7 @@ P = 128
 TOKENS = 1024
 TOKEN_TILES = TOKENS // P
 HID = 256
+HID_TILES = HID // P
 GATES = 4 * HID
 K_IN = 1536
 K_PASS = 512
@@ -24,6 +25,8 @@ BANK = 512
 BANKS = GATES // BANK
 ROW_TILES = 2
 STEP_COLS = ROW_TILES * P
+GT_STEPS = TOKENS // STEP_COLS
+W_CHUNKS = GATES // STEP_COLS
 
 FLOPS = 2 * TOKENS * (K_IN + HID) * 2 * GATES
 
@@ -37,14 +40,16 @@ def tile_dependency_pa_kernel(
     whh = (whh_f, whh_b)
     bih = (bih_f, bih_b)
     bhh = (bhh_f, bhh_b)
+    out_view = out.rearrange("(p t) c -> p t c", t=TOKEN_TILES)
 
     with ExitStack() as ctx:
+        ctx.enter_context(tc.manual_schedule())
         consts = ctx.enter_context(tc.tile_pool(name="consts", bufs=1))
         keep = ctx.enter_context(tc.tile_pool(name="keep", bufs=1))
         wih_pool = ctx.enter_context(tc.tile_pool(name="wih_pool", bufs=4))
         stage = ctx.enter_context(tc.tile_pool(name="stage", bufs=4))
-        flip_psum = ctx.enter_context(tc.psum_pool(name="flip_psum", bufs=3))
-        sum_psum = ctx.enter_context(tc.psum_pool(name="sum_psum", bufs=5))
+        cell_pool = ctx.enter_context(tc.tile_pool(name="cell_pool", bufs=3))
+        psum = ctx.enter_context(tc.psum_pool(name="psum", bufs=8))
 
         ident_bf = consts.tile([P, P], BF16)
         make_identity(nc, ident_bf[:])
@@ -52,12 +57,19 @@ def tile_dependency_pa_kernel(
         make_identity(nc, ident_f32[:])
         ones = consts.tile([P, P], BF16)
         nc.vector.memset(ones[:], 1.0)
+        bias_rows = consts.tile([P, 2 * GATES], BF16)
+        nc.vector.memset(bias_rows[:], 0.0)
+        for d in range(2):
+            nc.scalar.dma_start(out=bias_rows[0:1, d * GATES:(d + 1) * GATES], in_=bih[d].rearrange("(o n) -> o n", o=1))
+            nc.scalar.dma_start(out=bias_rows[1:2, d * GATES:(d + 1) * GATES], in_=bhh[d].rearrange("(o n) -> o n", o=1))
         warm = consts.tile([P, 1], F32)
         nc.vector.memset(warm[:], 0.0)
         nc.scalar.activation(out=warm[:], in_=warm[:], func=ACT.Sigmoid)
 
-        h0T = [keep.tile([P, HID // P, TOKENS], BF16, name="h0T%d" % d) for d in range(2)]
-        whhT = [keep.tile([P, HID // P, GATES], BF16, name="whhT%d" % d) for d in range(2)]
+        h0_raw = [keep.tile([P, TOKEN_TILES * HID], BF16, name="h0_raw%d" % d) for d in range(2)]
+        whh_raw = [keep.tile([P, TOKEN_TILES * HID], BF16, name="whh_raw%d" % d) for d in range(2)]
+        h0T = [keep.tile([P, HID_TILES, TOKENS], BF16, name="h0T%d" % d) for d in range(2)]
+        whhT = [keep.tile([P, HID_TILES, GATES], BF16, name="whhT%d" % d) for d in range(2)]
         c0_sb = [keep.tile([P, TOKEN_TILES, HID], BF16, name="c0_sb%d" % d) for d in range(2)]
         gt_raw = [keep.tile([P, TOKEN_TILES * K_PASS], BF16, name="gt_raw%d" % g) for g in range(PASSES)]
         gt_codes = keep.tile([P, PASSES, TOKENS], U32, align_bytes=64)
@@ -65,11 +77,43 @@ def tile_dependency_pa_kernel(
         w_codes = [keep.tile([P, PASSES, GATES], U32, align_bytes=64, name="w_codes%d" % d) for d in range(2)]
         w_scales = [keep.tile([P, PASSES, GATES], U8, align_bytes=64, name="w_scales%d" % d) for d in range(2)]
         gates = [keep.tile([P, TOKEN_TILES, GATES], F32, name="gates%d" % d) for d in range(2)]
-        bias_rows = consts.tile([P, 2 * GATES], BF16)
         bias_all = consts.tile([P, 2 * GATES], F32)
 
+        def load_hidden(d):
+            nc.sync.dma_start(out=h0_raw[d][:], in_=h0[d].rearrange("(p t) k -> p (t k)", t=TOKEN_TILES))
+            nc.sync.dma_start(
+                out=whh_raw[d][:].rearrange("p (t k) -> p t k", t=TOKEN_TILES),
+                in_=whh[d].rearrange("(t p) k -> p t k", p=P),
+            )
+
+        def transpose_hidden(raw, flat):
+            for kt in range(HID_TILES):
+                for half in range(2):
+                    flipped = psum.tile([P, 4, P], BF16, tag="bank")
+                    for i in range(4):
+                        first = (4 * half + i) * HID + kt * P
+                        nc.tensor.transpose(out=flipped[:, i, :], in_=raw[:, first:first + P], identity=ident_bf[:])
+                    nc.scalar.copy(out=flat[:, kt, 4 * half * P:4 * (half + 1) * P], in_=flipped[:].rearrange("p i r -> p (i r)"))
+
+        def hidden_bank(n):
+            if n >= 2 * TOKEN_TILES * BANKS:
+                return
+            d, rest = divmod(n, TOKEN_TILES * BANKS)
+            t, b = divmod(rest, BANKS)
+            cols = slice(b * BANK, (b + 1) * BANK)
+            acc = psum.tile([P, BANK], F32, tag="bank")
+            for kt in range(HID_TILES):
+                nc.tensor.matmul(
+                    out=acc[:], lhsT=h0T[d][:, kt, t * P:(t + 1) * P], rhs=whhT[d][:, kt, cols],
+                    start=(kt == 0), stop=(kt == HID_TILES - 1),
+                )
+            nc.vector.tensor_tensor(
+                out=gates[d][:, t, cols], in0=acc[:],
+                in1=bias_all[:, d * GATES + b * BANK:d * GATES + (b + 1) * BANK], op=ALU.add,
+            )
+
         def quantise_step(rows, codes, scales):
-            flipped = flip_psum.tile([P, ROW_TILES, 2, P], F32, tag="flipped")
+            flipped = psum.tile([P, ROW_TILES, 2, P], F32, tag="bank")
             for r in range(ROW_TILES):
                 for u in range(2):
                     nc.tensor.transpose(out=flipped[:, r, u, :], in_=rows[r][:, u * P:(u + 1) * P], identity=ident_f32[:])
@@ -80,119 +124,94 @@ def tile_dependency_pa_kernel(
             )
             nc.vector.quantize_mx(out=codes.bitcast(FP8X4), scales=scales, in_=grouped[:])
 
-        def transpose_hidden(raw, flat):
-            for kt in range(HID // P):
-                for half in range(2):
-                    flipped = flip_psum.tile([P, 4, P], BF16, tag="flipped")
-                    for i in range(4):
-                        first = (4 * half + i) * HID + kt * P
-                        nc.tensor.transpose(out=flipped[:, i, :], in_=raw[:, first:first + P], identity=ident_bf[:])
-                    nc.scalar.copy(out=flat[:, kt, 4 * half * P:4 * (half + 1) * P], in_=flipped[:].rearrange("p i r -> p (i r)"))
-
-        def hidden_product(d):
-            for t in range(TOKEN_TILES):
-                for b in range(BANKS):
-                    cols = slice(b * BANK, (b + 1) * BANK)
-                    acc = sum_psum.tile([P, BANK], F32, tag="acc")
-                    for kt in range(HID // P):
-                        nc.tensor.matmul(
-                            out=acc[:], lhsT=h0T[d][:, kt, t * P:(t + 1) * P], rhs=whhT[d][:, kt, cols],
-                            start=(kt == 0), stop=(kt == HID // P - 1),
-                        )
-                    nc.vector.tensor_tensor(
-                        out=gates[d][:, t, cols], in0=acc[:],
-                        in1=bias_all[:, d * GATES + b * BANK:d * GATES + (b + 1) * BANK], op=ALU.add,
-                    )
-
-        def quantise_weights(d):
-            chunks_of_rows = wih[d].rearrange("(c r p) k -> c p r k", r=ROW_TILES, p=P)
-            for c in range(GATES // STEP_COLS):
-                w_raw = wih_pool.tile([P, ROW_TILES * K_IN], BF16)
-                nc.sync.dma_start(out=w_raw[:].rearrange("p (r k) -> p r k", r=ROW_TILES), in_=chunks_of_rows[c])
-                words = w_raw[:].bitcast(F32)
-                for g in range(PASSES):
-                    firsts = [r * (K_IN // 2) + g * WORDS for r in range(ROW_TILES)]
-                    cols = slice(c * STEP_COLS, (c + 1) * STEP_COLS)
-                    quantise_step([words[:, f:f + WORDS] for f in firsts], w_codes[d][:, g, cols], w_scales[d][:, g, cols])
-
-        def lstm_direction(d):
-            out_view = out.rearrange("(p t) c -> p t c", t=TOKEN_TILES)
-            for pair in range(TOKEN_TILES // 2):
-                two = slice(2 * pair, 2 * pair + 2)
-                for b in range(BANKS):
-                    cols = slice(b * BANK, (b + 1) * BANK)
-                    for t in range(2 * pair, 2 * pair + 2):
-                        acc = sum_psum.tile([P, BANK], F32, tag="acc")
-                        for g in range(PASSES):
-                            nc.tensor.matmul_mx(
-                                out=acc[:],
-                                lhsT=gt_codes[:, g, t * P:(t + 1) * P].bitcast(FP8X4),
-                                lhsT_scale=gt_scales[:, g, t * P:(t + 1) * P],
-                                rhs=w_codes[d][:, g, cols].bitcast(FP8X4),
-                                rhs_scale=w_scales[d][:, g, cols],
-                                start=(g == 0), stop=(g == PASSES - 1),
-                            )
-                        nc.vector.tensor_tensor(out=gates[d][:, t, cols], in0=acc[:], in1=gates[d][:, t, cols], op=ALU.add)
-                gate_i = gates[d][:, two, 0:HID]
-                gate_f = gates[d][:, two, HID:2 * HID]
-                gate_g = gates[d][:, two, 2 * HID:3 * HID]
-                gate_o = gates[d][:, two, 3 * HID:4 * HID]
-                nc.scalar.activation(out=gates[d][:, two, 0:2 * HID], in_=gates[d][:, two, 0:2 * HID], func=ACT.Sigmoid)
-                nc.scalar.activation(out=gate_g, in_=gate_g, func=ACT.Tanh)
-                nc.scalar.activation(out=gate_o, in_=gate_o, func=ACT.Sigmoid)
-                kept = cell_pool.tile([P, 2, HID], F32)
-                nc.vector.tensor_tensor(out=kept[:], in0=gate_f, in1=c0_sb[d][:, two, :], op=ALU.mult)
-                fresh = cell_pool.tile([P, 2, HID], F32)
-                nc.vector.tensor_tensor(out=fresh[:], in0=gate_i, in1=gate_g, op=ALU.mult)
-                cell = cell_pool.tile([P, 2, HID], F32)
-                nc.vector.tensor_tensor(out=cell[:], in0=kept[:], in1=fresh[:], op=ALU.add)
-                nc.scalar.activation(out=cell[:], in_=cell[:], func=ACT.Tanh)
-                hidden = cell_pool.tile([P, 2, HID], F32)
-                nc.vector.tensor_tensor(out=hidden[:], in0=gate_o, in1=cell[:], op=ALU.mult)
-                nc.sync.dma_start(out=out_view[:, two, d * HID:(d + 1) * HID], in_=hidden[:])
-
-        with tc.tile_pool(name="hidden_raw", bufs=1) as hidden_raw:
-            h0_raw = [hidden_raw.tile([P, TOKEN_TILES * HID], BF16, name="h0_raw%d" % d) for d in range(2)]
-            whh_raw = [hidden_raw.tile([P, TOKEN_TILES * HID], BF16, name="whh_raw%d" % d) for d in range(2)]
-            nc.vector.memset(bias_rows[:], 0.0)
-            for d in range(2):
-                nc.scalar.dma_start(out=bias_rows[0:1, d * GATES:(d + 1) * GATES], in_=bih[d].rearrange("(o n) -> o n", o=1))
-                nc.scalar.dma_start(out=bias_rows[1:2, d * GATES:(d + 1) * GATES], in_=bhh[d].rearrange("(o n) -> o n", o=1))
-            for d in range(2):
-                nc.sync.dma_start(out=h0_raw[d][:], in_=h0[d].rearrange("(p t) k -> p (t k)", t=TOKEN_TILES))
-                nc.sync.dma_start(
-                    out=whh_raw[d][:].rearrange("p (t k) -> p t k", t=TOKEN_TILES),
-                    in_=whh[d].rearrange("(t p) k -> p t k", p=P),
+        def input_bank(d, t, b):
+            cols = slice(b * BANK, (b + 1) * BANK)
+            acc = psum.tile([P, BANK], F32, tag="bank")
+            for g in range(PASSES):
+                nc.tensor.matmul_mx(
+                    out=acc[:],
+                    lhsT=gt_codes[:, g, t * P:(t + 1) * P].bitcast(FP8X4),
+                    lhsT_scale=gt_scales[:, g, t * P:(t + 1) * P],
+                    rhs=w_codes[d][:, g, cols].bitcast(FP8X4),
+                    rhs_scale=w_scales[d][:, g, cols],
+                    start=(g == 0), stop=(g == PASSES - 1),
                 )
-            nc.sync.dma_start(out=gt_raw[0][:], in_=hn_chunks.rearrange("(p t) k -> p (t k)", t=TOKEN_TILES))
-            nc.sync.dma_start(out=gt_raw[1][:], in_=hn_tags.rearrange("(p t) k -> p (t k)", t=TOKEN_TILES))
-            last_pass = gt_raw[2][:].rearrange("p (t k) -> p t k", t=TOKEN_TILES)
-            first = 0
-            for stream in (x, tags, chunks):
-                width = stream.shape[1]
-                nc.sync.dma_start(out=last_pass[:, :, first:first + width], in_=stream.rearrange("(p t) k -> p t k", t=TOKEN_TILES))
-                first += width
+            nc.vector.tensor_tensor(out=gates[d][:, t, cols], in0=acc[:], in1=gates[d][:, t, cols], op=ALU.add)
 
-            for q in range(2 * BANKS):
-                acc = sum_psum.tile([P, BANK], F32, tag="acc")
-                nc.tensor.matmul(out=acc[:], lhsT=ones[:], rhs=bias_rows[:, q * BANK:(q + 1) * BANK], start=True, stop=True)
-                nc.vector.tensor_copy(out=bias_all[:, q * BANK:(q + 1) * BANK], in_=acc[:])
-            for d in range(2):
-                transpose_hidden(h0_raw[d], h0T[d])
-                transpose_hidden(whh_raw[d], whhT[d])
+        def gate(d, t, first, count=1):
+            return gates[d][:, t, first * HID:(first + count) * HID]
 
-        cell_pool = ctx.enter_context(tc.tile_pool(name="cell_pool", bufs=2))
-        hidden_product(0)
+        load_hidden(0)
+        nc.sync.dma_start(out=gt_raw[0][:], in_=hn_chunks.rearrange("(p t) k -> p (t k)", t=TOKEN_TILES))
+        nc.sync.dma_start(out=gt_raw[1][:], in_=hn_tags.rearrange("(p t) k -> p (t k)", t=TOKEN_TILES))
+        last_pass = gt_raw[2][:].rearrange("p (t k) -> p t k", t=TOKEN_TILES)
+        first = 0
+        for stream in (x, tags, chunks):
+            width = stream.shape[1]
+            nc.sync.dma_start(out=last_pass[:, :, first:first + width], in_=stream.rearrange("(p t) k -> p t k", t=TOKEN_TILES))
+            first += width
+        load_hidden(1)
+
+        transpose_hidden(h0_raw[0], h0T[0])
+        transpose_hidden(whh_raw[0], whhT[0])
+        for q in range(2 * BANKS):
+            acc = psum.tile([P, BANK], F32, tag="bank")
+            nc.tensor.matmul(out=acc[:], lhsT=ones[:], rhs=bias_rows[:, q * BANK:(q + 1) * BANK], start=True, stop=True)
+            nc.scalar.copy(out=bias_all[:, q * BANK:(q + 1) * BANK], in_=acc[:])
         for g in range(PASSES):
             words = gt_raw[g][:].bitcast(F32)
-            for s in range(TOKENS // STEP_COLS):
+            for s in range(GT_STEPS):
+                hidden_bank(g * GT_STEPS + s)
                 cols = slice(s * STEP_COLS, (s + 1) * STEP_COLS)
                 firsts = [(ROW_TILES * s + r) * WORDS for r in range(ROW_TILES)]
                 quantise_step([words[:, f:f + WORDS] for f in firsts], gt_codes[:, g, cols], gt_scales[:, g, cols])
-        quantise_weights(0)
+        transpose_hidden(h0_raw[1], h0T[1])
+        transpose_hidden(whh_raw[1], whhT[1])
         for d in range(2):
+            chunks_of_rows = wih[d].rearrange("(c r p) k -> c p r k", r=ROW_TILES, p=P)
+            for c in range(W_CHUNKS):
+                w_raw = wih_pool.tile([P, ROW_TILES * K_IN], BF16)
+                nc.sync.dma_start(out=w_raw[:].rearrange("p (r k) -> p r k", r=ROW_TILES), in_=chunks_of_rows[c])
+                words = w_raw[:].bitcast(F32)
+                cols = slice(c * STEP_COLS, (c + 1) * STEP_COLS)
+                for g in range(PASSES):
+                    hidden_bank(PASSES * GT_STEPS + (d * W_CHUNKS + c) * PASSES + g)
+                    firsts = [r * (K_IN // 2) + g * WORDS for r in range(ROW_TILES)]
+                    quantise_step([words[:, f:f + WORDS] for f in firsts], w_codes[d][:, g, cols], w_scales[d][:, g, cols])
             nc.sync.dma_start(out=c0_sb[d][:], in_=c0[d].rearrange("(p t) k -> p t k", t=TOKEN_TILES))
-        hidden_product(1)
-        quantise_weights(1)
-        lstm_direction(0)
-        lstm_direction(1)
+
+        units = [(d, t) for d in range(2) for t in range(TOKEN_TILES)]
+        kept = {}
+        fresh = {}
+        cell = {}
+
+        def activate_gates(n):
+            d, t = units[n]
+            input_bank(d, t, 0)
+            nc.scalar.activation(out=gate(d, t, 0, 2), in_=gate(d, t, 0, 2), func=ACT.Sigmoid)
+            kept[n] = cell_pool.tile([P, HID], F32, name="kept")
+            nc.gpsimd.tensor_tensor(out=kept[n][:], in0=gate(d, t, 1), in1=c0_sb[d][:, t, :], op=ALU.mult)
+            input_bank(d, t, 1)
+            nc.scalar.activation(out=gate(d, t, 2), in_=gate(d, t, 2), func=ACT.Tanh)
+            nc.scalar.activation(out=gate(d, t, 3), in_=gate(d, t, 3), func=ACT.Sigmoid)
+            fresh[n] = cell_pool.tile([P, HID], F32, name="fresh")
+            nc.gpsimd.tensor_tensor(out=fresh[n][:], in0=gate(d, t, 0), in1=gate(d, t, 2), op=ALU.mult)
+
+        def new_cell(n):
+            cell[n] = cell_pool.tile([P, HID], F32, name="cell")
+            nc.vector.tensor_tensor(out=cell[n][:], in0=kept[n][:], in1=fresh[n][:], op=ALU.add)
+            nc.scalar.activation(out=cell[n][:], in_=cell[n][:], func=ACT.Tanh)
+
+        def new_hidden(n):
+            d, t = units[n]
+            hidden = cell_pool.tile([P, HID], F32, name="hidden")
+            nc.vector.tensor_tensor(out=hidden[:], in0=gate(d, t, 3), in1=cell[n][:], op=ALU.mult)
+            nc.sync.dma_start(out=out_view[:, t, d * HID:(d + 1) * HID], in_=hidden[:])
+
+        for n in range(len(units) + 2):
+            if n < len(units):
+                activate_gates(n)
+            if 1 <= n <= len(units):
+                new_cell(n - 1)
+            if n >= 2:
+                new_hidden(n - 2)

@@ -27,6 +27,7 @@ ROW_TILES = 2
 STEP_COLS = ROW_TILES * P
 GT_STEPS = TOKENS // STEP_COLS
 W_CHUNKS = GATES // STEP_COLS
+SCALAR_EVERY = 4
 
 FLOPS = 2 * TOKENS * (K_IN + HID) * 2 * GATES
 
@@ -101,16 +102,19 @@ def tile_dependency_pa_kernel(
             d, rest = divmod(n, TOKEN_TILES * BANKS)
             t, b = divmod(rest, BANKS)
             cols = slice(b * BANK, (b + 1) * BANK)
+            bias_cols = slice(d * GATES + b * BANK, d * GATES + (b + 1) * BANK)
+            by_scalar = n % SCALAR_EVERY == SCALAR_EVERY - 1
             acc = psum.tile([P, BANK], F32, tag="bank")
             for kt in range(HID_TILES):
                 nc.tensor.matmul(
                     out=acc[:], lhsT=h0T[d][:, kt, t * P:(t + 1) * P], rhs=whhT[d][:, kt, cols],
-                    start=(kt == 0), stop=(kt == HID_TILES - 1),
+                    start=(kt == 0), stop=(kt == HID_TILES - 1 and not by_scalar),
                 )
-            nc.vector.tensor_tensor(
-                out=gates[d][:, t, cols], in0=acc[:],
-                in1=bias_all[:, d * GATES + b * BANK:d * GATES + (b + 1) * BANK], op=ALU.add,
-            )
+            if by_scalar:
+                nc.tensor.matmul(out=acc[:], lhsT=ones[:], rhs=bias_rows[:, bias_cols], start=False, stop=True)
+                nc.scalar.copy(out=gates[d][:, t, cols], in_=acc[:])
+            else:
+                nc.vector.tensor_tensor(out=gates[d][:, t, cols], in0=acc[:], in1=bias_all[:, bias_cols], op=ALU.add)
 
         def quantise_step(rows, codes, scales):
             flipped = psum.tile([P, ROW_TILES, 2, P], F32, tag="bank")
@@ -153,11 +157,11 @@ def tile_dependency_pa_kernel(
         load_hidden(1)
 
         transpose_hidden(h0_raw[0], h0T[0])
-        transpose_hidden(whh_raw[0], whhT[0])
         for q in range(2 * BANKS):
             acc = psum.tile([P, BANK], F32, tag="bank")
             nc.tensor.matmul(out=acc[:], lhsT=ones[:], rhs=bias_rows[:, q * BANK:(q + 1) * BANK], start=True, stop=True)
-            nc.scalar.copy(out=bias_all[:, q * BANK:(q + 1) * BANK], in_=acc[:])
+            nc.vector.tensor_copy(out=bias_all[:, q * BANK:(q + 1) * BANK], in_=acc[:])
+        transpose_hidden(whh_raw[0], whhT[0])
         for g in range(PASSES):
             words = gt_raw[g][:].bitcast(F32)
             for s in range(GT_STEPS):

@@ -49,7 +49,7 @@ def tile_dependency_pa_kernel(
         keep = ctx.enter_context(tc.tile_pool(name="keep", bufs=1))
         wih_pool = ctx.enter_context(tc.tile_pool(name="wih_pool", bufs=4))
         stage = ctx.enter_context(tc.tile_pool(name="stage", bufs=4))
-        cell_pool = ctx.enter_context(tc.tile_pool(name="cell_pool", bufs=3))
+        cell_pool = ctx.enter_context(tc.tile_pool(name="cell_pool", bufs=4))
         psum = ctx.enter_context(tc.psum_pool(name="psum", bufs=8))
 
         ident_bf = consts.tile([P, P], BF16)
@@ -198,8 +198,11 @@ def tile_dependency_pa_kernel(
             input_bank(d, t, 1)
             nc.scalar.activation(out=gate(d, t, 2), in_=gate(d, t, 2), func=ACT.Tanh)
             nc.scalar.activation(out=gate(d, t, 3), in_=gate(d, t, 3), func=ACT.Sigmoid)
+
+        def fresh_part(n):
+            d, t = units[n]
             fresh[n] = cell_pool.tile([P, HID], F32, name="fresh")
-            nc.gpsimd.tensor_tensor(out=fresh[n][:], in0=gate(d, t, 0), in1=gate(d, t, 2), op=ALU.mult)
+            nc.vector.tensor_tensor(out=fresh[n][:], in0=gate(d, t, 0), in1=gate(d, t, 2), op=ALU.mult)
 
         def new_cell(n):
             cell[n] = cell_pool.tile([P, HID], F32, name="cell")
@@ -212,10 +215,8 @@ def tile_dependency_pa_kernel(
             nc.vector.tensor_tensor(out=hidden[:], in0=gate(d, t, 3), in1=cell[n][:], op=ALU.mult)
             nc.sync.dma_start(out=out_view[:, t, d * HID:(d + 1) * HID], in_=hidden[:])
 
-        for n in range(len(units) + 2):
-            if n < len(units):
-                activate_gates(n)
-            if 1 <= n <= len(units):
-                new_cell(n - 1)
-            if n >= 2:
-                new_hidden(n - 2)
+        stages = (activate_gates, fresh_part, new_cell, new_hidden)
+        for n in range(len(units) + len(stages) - 1):
+            for lag, stage_of in enumerate(stages):
+                if 0 <= n - lag < len(units):
+                    stage_of(n - lag)

@@ -96,31 +96,29 @@ def tile_dependency_pa_kernel(
                         nc.tensor.transpose(out=flipped[:, i, :], in_=raw[:, first:first + P], identity=ident_bf[:])
                     nc.scalar.copy(out=flat[:, kt, 4 * half * P:4 * (half + 1) * P], in_=flipped[:].rearrange("p i r -> p (i r)"))
 
-        def hidden_bank(n):
-            if n >= 2 * TOKEN_TILES * BANKS:
-                return
+        def bank_and_step(n, rows, codes, scales):
+            with_bank = n < 2 * TOKEN_TILES * BANKS
             d, rest = divmod(n, TOKEN_TILES * BANKS)
             t, b = divmod(rest, BANKS)
             cols = slice(b * BANK, (b + 1) * BANK)
             bias_cols = slice(d * GATES + b * BANK, d * GATES + (b + 1) * BANK)
             by_scalar = n % SCALAR_EVERY == SCALAR_EVERY - 1
-            acc = psum.tile([P, BANK], F32, tag="bank")
-            for kt in range(HID_TILES):
-                nc.tensor.matmul(
-                    out=acc[:], lhsT=h0T[d][:, kt, t * P:(t + 1) * P], rhs=whhT[d][:, kt, cols],
-                    start=(kt == 0), stop=(kt == HID_TILES - 1 and not by_scalar),
-                )
-            if by_scalar:
+            if with_bank:
+                acc = psum.tile([P, BANK], F32, tag="bank")
+            flipped = psum.tile([P, ROW_TILES, 2, P], F32, tag="bank")
+            for half in range(2):
+                if with_bank:
+                    nc.tensor.matmul(
+                        out=acc[:], lhsT=h0T[d][:, half, t * P:(t + 1) * P], rhs=whhT[d][:, half, cols],
+                        start=(half == 0), stop=(half == 1 and not by_scalar),
+                    )
+                for u in range(2):
+                    nc.tensor.transpose(out=flipped[:, half, u, :], in_=rows[half][:, u * P:(u + 1) * P], identity=ident_f32[:])
+            if with_bank and by_scalar:
                 nc.tensor.matmul(out=acc[:], lhsT=ones[:], rhs=bias_rows[:, bias_cols], start=False, stop=True)
                 nc.scalar.copy(out=gates[d][:, t, cols], in_=acc[:])
-            else:
+            elif with_bank:
                 nc.vector.tensor_tensor(out=gates[d][:, t, cols], in0=acc[:], in1=bias_all[:, bias_cols], op=ALU.add)
-
-        def quantise_step(rows, codes, scales):
-            flipped = psum.tile([P, ROW_TILES, 2, P], F32, tag="bank")
-            for r in range(ROW_TILES):
-                for u in range(2):
-                    nc.tensor.transpose(out=flipped[:, r, u, :], in_=rows[r][:, u * P:(u + 1) * P], identity=ident_f32[:])
             grouped = stage.tile([P, 4 * STEP_COLS], BF16, align_bytes=64)
             nc.scalar.copy(
                 out=grouped[:].bitcast(F32).rearrange("p (r c u) -> p r c u", r=ROW_TILES, u=2),
@@ -165,10 +163,9 @@ def tile_dependency_pa_kernel(
         for g in range(PASSES):
             words = gt_raw[g][:].bitcast(F32)
             for s in range(GT_STEPS):
-                hidden_bank(g * GT_STEPS + s)
                 cols = slice(s * STEP_COLS, (s + 1) * STEP_COLS)
                 firsts = [(ROW_TILES * s + r) * WORDS for r in range(ROW_TILES)]
-                quantise_step([words[:, f:f + WORDS] for f in firsts], gt_codes[:, g, cols], gt_scales[:, g, cols])
+                bank_and_step(g * GT_STEPS + s, [words[:, f:f + WORDS] for f in firsts], gt_codes[:, g, cols], gt_scales[:, g, cols])
         transpose_hidden(h0_raw[1], h0T[1])
         transpose_hidden(whh_raw[1], whhT[1])
         for d in range(2):
@@ -179,9 +176,11 @@ def tile_dependency_pa_kernel(
                 words = w_raw[:].bitcast(F32)
                 cols = slice(c * STEP_COLS, (c + 1) * STEP_COLS)
                 for g in range(PASSES):
-                    hidden_bank(PASSES * GT_STEPS + (d * W_CHUNKS + c) * PASSES + g)
                     firsts = [r * (K_IN // 2) + g * WORDS for r in range(ROW_TILES)]
-                    quantise_step([words[:, f:f + WORDS] for f in firsts], w_codes[d][:, g, cols], w_scales[d][:, g, cols])
+                    bank_and_step(
+                        PASSES * GT_STEPS + (d * W_CHUNKS + c) * PASSES + g,
+                        [words[:, f:f + WORDS] for f in firsts], w_codes[d][:, g, cols], w_scales[d][:, g, cols],
+                    )
             nc.sync.dma_start(out=c0_sb[d][:], in_=c0[d].rearrange("(p t) k -> p t k", t=TOKEN_TILES))
 
         units = [(d, t) for d in range(2) for t in range(TOKEN_TILES)]

@@ -44,7 +44,6 @@ def tile_dependency_pa_kernel(
     out_view = out.rearrange("(p t) c -> p t c", t=TOKEN_TILES)
 
     with ExitStack() as ctx:
-        ctx.enter_context(tc.manual_schedule())
         consts = ctx.enter_context(tc.tile_pool(name="consts", bufs=1))
         keep = ctx.enter_context(tc.tile_pool(name="keep", bufs=1))
         wih_pool = ctx.enter_context(tc.tile_pool(name="wih_pool", bufs=4))
@@ -96,29 +95,31 @@ def tile_dependency_pa_kernel(
                         nc.tensor.transpose(out=flipped[:, i, :], in_=raw[:, first:first + P], identity=ident_bf[:])
                     nc.scalar.copy(out=flat[:, kt, 4 * half * P:4 * (half + 1) * P], in_=flipped[:].rearrange("p i r -> p (i r)"))
 
-        def bank_and_step(n, rows, codes, scales):
-            with_bank = n < 2 * TOKEN_TILES * BANKS
+        def hidden_bank(n):
+            if n >= 2 * TOKEN_TILES * BANKS:
+                return
             d, rest = divmod(n, TOKEN_TILES * BANKS)
             t, b = divmod(rest, BANKS)
             cols = slice(b * BANK, (b + 1) * BANK)
             bias_cols = slice(d * GATES + b * BANK, d * GATES + (b + 1) * BANK)
             by_scalar = n % SCALAR_EVERY == SCALAR_EVERY - 1
-            if with_bank:
-                acc = psum.tile([P, BANK], F32, tag="bank")
-            flipped = psum.tile([P, ROW_TILES, 2, P], F32, tag="bank")
-            for half in range(2):
-                if with_bank:
-                    nc.tensor.matmul(
-                        out=acc[:], lhsT=h0T[d][:, half, t * P:(t + 1) * P], rhs=whhT[d][:, half, cols],
-                        start=(half == 0), stop=(half == 1 and not by_scalar),
-                    )
-                for u in range(2):
-                    nc.tensor.transpose(out=flipped[:, half, u, :], in_=rows[half][:, u * P:(u + 1) * P], identity=ident_f32[:])
-            if with_bank and by_scalar:
+            acc = psum.tile([P, BANK], F32, tag="bank")
+            for kt in range(HID_TILES):
+                nc.tensor.matmul(
+                    out=acc[:], lhsT=h0T[d][:, kt, t * P:(t + 1) * P], rhs=whhT[d][:, kt, cols],
+                    start=(kt == 0), stop=(kt == HID_TILES - 1 and not by_scalar),
+                )
+            if by_scalar:
                 nc.tensor.matmul(out=acc[:], lhsT=ones[:], rhs=bias_rows[:, bias_cols], start=False, stop=True)
                 nc.scalar.copy(out=gates[d][:, t, cols], in_=acc[:])
-            elif with_bank:
+            else:
                 nc.vector.tensor_tensor(out=gates[d][:, t, cols], in0=acc[:], in1=bias_all[:, bias_cols], op=ALU.add)
+
+        def quantise_step(rows, codes, scales):
+            flipped = psum.tile([P, ROW_TILES, 2, P], F32, tag="bank")
+            for r in range(ROW_TILES):
+                for u in range(2):
+                    nc.tensor.transpose(out=flipped[:, r, u, :], in_=rows[r][:, u * P:(u + 1) * P], identity=ident_f32[:])
             grouped = stage.tile([P, 4 * STEP_COLS], BF16, align_bytes=64)
             nc.scalar.copy(
                 out=grouped[:].bitcast(F32).rearrange("p (r c u) -> p r c u", r=ROW_TILES, u=2),
@@ -163,9 +164,10 @@ def tile_dependency_pa_kernel(
         for g in range(PASSES):
             words = gt_raw[g][:].bitcast(F32)
             for s in range(GT_STEPS):
+                hidden_bank(g * GT_STEPS + s)
                 cols = slice(s * STEP_COLS, (s + 1) * STEP_COLS)
                 firsts = [(ROW_TILES * s + r) * WORDS for r in range(ROW_TILES)]
-                bank_and_step(g * GT_STEPS + s, [words[:, f:f + WORDS] for f in firsts], gt_codes[:, g, cols], gt_scales[:, g, cols])
+                quantise_step([words[:, f:f + WORDS] for f in firsts], gt_codes[:, g, cols], gt_scales[:, g, cols])
         transpose_hidden(h0_raw[1], h0T[1])
         transpose_hidden(whh_raw[1], whhT[1])
         for d in range(2):
@@ -176,11 +178,9 @@ def tile_dependency_pa_kernel(
                 words = w_raw[:].bitcast(F32)
                 cols = slice(c * STEP_COLS, (c + 1) * STEP_COLS)
                 for g in range(PASSES):
+                    hidden_bank(PASSES * GT_STEPS + (d * W_CHUNKS + c) * PASSES + g)
                     firsts = [r * (K_IN // 2) + g * WORDS for r in range(ROW_TILES)]
-                    bank_and_step(
-                        PASSES * GT_STEPS + (d * W_CHUNKS + c) * PASSES + g,
-                        [words[:, f:f + WORDS] for f in firsts], w_codes[d][:, g, cols], w_scales[d][:, g, cols],
-                    )
+                    quantise_step([words[:, f:f + WORDS] for f in firsts], w_codes[d][:, g, cols], w_scales[d][:, g, cols])
             nc.sync.dma_start(out=c0_sb[d][:], in_=c0[d].rearrange("(p t) k -> p t k", t=TOKEN_TILES))
 
         units = [(d, t) for d in range(2) for t in range(TOKEN_TILES)]

from contextlib import ExitStack

import concourse.mybir as mybir
from concourse.masks import make_identity

F32 = mybir.dt.float32
BF16 = mybir.dt.bfloat16
U32 = mybir.dt.uint32
U8 = mybir.dt.uint8
FP8X4 = mybir.dt.float8_e4m3fn_x4
ACT = mybir.ActivationFunctionType
ALU = mybir.AluOpType

P = 128
TOKENS = 1024
TOKEN_TILES = TOKENS // P
HID = 256
HID_TILES = HID // P
GATES = 4 * HID
K_IN = 1536
K_PASS = 512
PASSES = K_IN // K_PASS
WORDS = K_PASS // 2
BANK = 512
BANKS = GATES // BANK
ROW_TILES = 2
STEP_COLS = ROW_TILES * P
GT_STEPS = TOKENS // STEP_COLS
W_CHUNKS = GATES // STEP_COLS
SCALAR_EVERY = 4

FLOPS = 2 * TOKENS * (K_IN + HID) * 2 * GATES


def tile_dependency_pa_kernel(
    tc, hn_chunks, hn_tags, x, tags, chunks, h0, c0,
    wih_f, whh_f, bih_f, bhh_f, wih_b, whh_b, bih_b, bhh_b, out,
):
    nc = tc.nc
    wih = (wih_f, wih_b)
    whh = (whh_f, whh_b)
    bih = (bih_f, bih_b)
    bhh = (bhh_f, bhh_b)
    out_view = out.rearrange("(p t) c -> p t c", t=TOKEN_TILES)

    with ExitStack() as ctx:
        consts = ctx.enter_context(tc.tile_pool(name="consts", bufs=1))
        keep = ctx.enter_context(tc.tile_pool(name="keep", bufs=1))
        wih_pool = ctx.enter_context(tc.tile_pool(name="wih_pool", bufs=4))
        stage = ctx.enter_context(tc.tile_pool(name="stage", bufs=4))
        cell_pool = ctx.enter_context(tc.tile_pool(name="cell_pool", bufs=4))
        psum = ctx.enter_context(tc.psum_pool(name="psum", bufs=8))

        ident_bf = consts.tile([P, P], BF16)
        make_identity(nc, ident_bf[:])
        ident_f32 = consts.tile([P, P], F32)
        make_identity(nc, ident_f32[:])
        ones = consts.tile([P, P], BF16)
        nc.vector.memset(ones[:], 1.0)
        bias_rows = consts.tile([P, 2 * GATES], BF16)
        nc.vector.memset(bias_rows[:], 0.0)
        for d in range(2):
            nc.scalar.dma_start(out=bias_rows[0:1, d * GATES:(d + 1) * GATES], in_=bih[d].rearrange("(o n) -> o n", o=1))
            nc.scalar.dma_start(out=bias_rows[1:2, d * GATES:(d + 1) * GATES], in_=bhh[d].rearrange("(o n) -> o n", o=1))
        warm = consts.tile([P, 1], F32)
        nc.vector.memset(warm[:], 0.0)
        nc.scalar.activation(out=warm[:], in_=warm[:], func=ACT.Sigmoid)

        h0_raw = [keep.tile([P, TOKEN_TILES * HID], BF16, name="h0_raw%d" % d) for d in range(2)]
        whh_raw = [keep.tile([P, TOKEN_TILES * HID], BF16, name="whh_raw%d" % d) for d in range(2)]
        h0T = [keep.tile([P, HID_TILES, TOKENS], BF16, name="h0T%d" % d) for d in range(2)]
        whhT = [keep.tile([P, HID_TILES, GATES], BF16, name="whhT%d" % d) for d in range(2)]
        c0_sb = [keep.tile([P, TOKEN_TILES, HID], BF16, name="c0_sb%d" % d) for d in range(2)]
        gt_raw = [keep.tile([P, TOKEN_TILES * K_PASS], BF16, name="gt_raw%d" % g) for g in range(PASSES)]
        gt_codes = keep.tile([P, PASSES, TOKENS], U32, align_bytes=64)
        gt_scales = keep.tile([P, PASSES, TOKENS], U8, align_bytes=64)
        w_codes = [keep.tile([P, PASSES, GATES], U32, align_bytes=64, name="w_codes%d" % d) for d in range(2)]
        w_scales = [keep.tile([P, PASSES, GATES], U8, align_bytes=64, name="w_scales%d" % d) for d in range(2)]
        gates = [keep.tile([P, TOKEN_TILES, GATES], F32, name="gates%d" % d) for d in range(2)]
        bias_all = consts.tile([P, 2 * GATES], F32)

        def load_hidden(d):
            nc.sync.dma_start(out=h0_raw[d][:], in_=h0[d].rearrange("(p t) k -> p (t k)", t=TOKEN_TILES))
            nc.sync.dma_start(
                out=whh_raw[d][:].rearrange("p (t k) -> p t k", t=TOKEN_TILES),
                in_=whh[d].rearrange("(t p) k -> p t k", p=P),
            )

        def transpose_hidden(raw, flat):
            for kt in range(HID_TILES):
                for half in range(2):
                    flipped = psum.tile([P, 4, P], BF16, tag="bank")
                    for i in range(4):
                        first = (4 * half + i) * HID + kt * P
                        nc.tensor.transpose(out=flipped[:, i, :], in_=raw[:, first:first + P], identity=ident_bf[:])
                    nc.scalar.copy(out=flat[:, kt, 4 * half * P:4 * (half + 1) * P], in_=flipped[:].rearrange("p i r -> p (i r)"))

        def hidden_bank(n):
            if n >= 2 * TOKEN_TILES * BANKS:
                return
            d, rest = divmod(n, TOKEN_TILES * BANKS)
            t, b = divmod(rest, BANKS)
            cols = slice(b * BANK, (b + 1) * BANK)
            bias_cols = slice(d * GATES + b * BANK, d * GATES + (b + 1) * BANK)
            by_scalar = n % SCALAR_EVERY == SCALAR_EVERY - 1
            acc = psum.tile([P, BANK], F32, tag="bank")
            for kt in range(HID_TILES):
                nc.tensor.matmul(
                    out=acc[:], lhsT=h0T[d][:, kt, t * P:(t + 1) * P], rhs=whhT[d][:, kt, cols],
                    start=(kt == 0), stop=(kt == HID_TILES - 1 and not by_scalar),
                )
            if by_scalar:
                nc.tensor.matmul(out=acc[:], lhsT=ones[:], rhs=bias_rows[:, bias_cols], start=False, stop=True)
                nc.scalar.copy(out=gates[d][:, t, cols], in_=acc[:])
            else:
                nc.vector.tensor_tensor(out=gates[d][:, t, cols], in0=acc[:], in1=bias_all[:, bias_cols], op=ALU.add)

        def quantise_step(rows, codes, scales):
            flipped = psum.tile([P, ROW_TILES, 2, P], F32, tag="bank")
            for r in range(ROW_TILES):
                for u in range(2):
                    nc.tensor.transpose(out=flipped[:, r, u, :], in_=rows[r][:, u * P:(u + 1) * P], identity=ident_f32[:])
            grouped = stage.tile([P, 4 * STEP_COLS], BF16, align_bytes=64)
            nc.scalar.copy(
                out=grouped[:].bitcast(F32).rearrange("p (r c u) -> p r c u", r=ROW_TILES, u=2),
                in_=flipped[:].rearrange("p r u c -> p r c u"),
            )
            nc.vector.quantize_mx(out=codes.bitcast(FP8X4), scales=scales, in_=grouped[:])

        def input_bank(d, t, b):
            cols = slice(b * BANK, (b + 1) * BANK)
            acc = psum.tile([P, BANK], F32, tag="bank")
            for g in range(PASSES):
                nc.tensor.matmul_mx(
                    out=acc[:],
                    lhsT=gt_codes[:, g, t * P:(t + 1) * P].bitcast(FP8X4),
                    lhsT_scale=gt_scales[:, g, t * P:(t + 1) * P],
                    rhs=w_codes[d][:, g, cols].bitcast(FP8X4),
                    rhs_scale=w_scales[d][:, g, cols],
                    start=(g == 0), stop=(g == PASSES - 1),
                )
            nc.vector.tensor_tensor(out=gates[d][:, t, cols], in0=acc[:], in1=gates[d][:, t, cols], op=ALU.add)

        def gate(d, t, first, count=1):
            return gates[d][:, t, first * HID:(first + count) * HID]

        load_hidden(0)
        nc.sync.dma_start(out=gt_raw[0][:], in_=hn_chunks.rearrange("(p t) k -> p (t k)", t=TOKEN_TILES))
        nc.sync.dma_start(out=gt_raw[1][:], in_=hn_tags.rearrange("(p t) k -> p (t k)", t=TOKEN_TILES))
        last_pass = gt_raw[2][:].rearrange("p (t k) -> p t k", t=TOKEN_TILES)
        first = 0
        for stream in (x, tags, chunks):
            width = stream.shape[1]
            nc.sync.dma_start(out=last_pass[:, :, first:first + width], in_=stream.rearrange("(p t) k -> p t k", t=TOKEN_TILES))
            first += width
        load_hidden(1)

        transpose_hidden(h0_raw[0], h0T[0])
        for q in range(2 * BANKS):
            acc = psum.tile([P, BANK], F32, tag="bank")
            nc.tensor.matmul(out=acc[:], lhsT=ones[:], rhs=bias_rows[:, q * BANK:(q + 1) * BANK], start=True, stop=True)
            nc.vector.tensor_copy(out=bias_all[:, q * BANK:(q + 1) * BANK], in_=acc[:])
        transpose_hidden(whh_raw[0], whhT[0])
        for g in range(PASSES):
            words = gt_raw[g][:].bitcast(F32)
            for s in range(GT_STEPS):
                hidden_bank(g * GT_STEPS + s)
                cols = slice(s * STEP_COLS, (s + 1) * STEP_COLS)
                firsts = [(ROW_TILES * s + r) * WORDS for r in range(ROW_TILES)]
                quantise_step([words[:, f:f + WORDS] for f in firsts], gt_codes[:, g, cols], gt_scales[:, g, cols])
        transpose_hidden(h0_raw[1], h0T[1])
        transpose_hidden(whh_raw[1], whhT[1])
        for d in range(2):
            chunks_of_rows = wih[d].rearrange("(c r p) k -> c p r k", r=ROW_TILES, p=P)
            for c in range(W_CHUNKS):
                w_raw = wih_pool.tile([P, ROW_TILES * K_IN], BF16)
                nc.sync.dma_start(out=w_raw[:].rearrange("p (r k) -> p r k", r=ROW_TILES), in_=chunks_of_rows[c])
                words = w_raw[:].bitcast(F32)
                cols = slice(c * STEP_COLS, (c + 1) * STEP_COLS)
                for g in range(PASSES):
                    hidden_bank(PASSES * GT_STEPS + (d * W_CHUNKS + c) * PASSES + g)
                    firsts = [r * (K_IN // 2) + g * WORDS for r in range(ROW_TILES)]
                    quantise_step([words[:, f:f + WORDS] for f in firsts], w_codes[d][:, g, cols], w_scales[d][:, g, cols])
            nc.sync.dma_start(out=c0_sb[d][:], in_=c0[d].rearrange("(p t) k -> p t k", t=TOKEN_TILES))

        units = [(d, t) for d in range(2) for t in range(TOKEN_TILES)]
        kept = {}
        fresh = {}
        cell = {}

        def activate_gates(n):
            d, t = units[n]
            input_bank(d, t, 0)
            nc.scalar.activation(out=gate(d, t, 0, 2), in_=gate(d, t, 0, 2), func=ACT.Sigmoid)
            kept[n] = cell_pool.tile([P, HID], F32, name="kept")
            nc.gpsimd.tensor_tensor(out=kept[n][:], in0=gate(d, t, 1), in1=c0_sb[d][:, t, :], op=ALU.mult)
            input_bank(d, t, 1)
            nc.scalar.activation(out=gate(d, t, 2), in_=gate(d, t, 2), func=ACT.Tanh)
            nc.scalar.activation(out=gate(d, t, 3), in_=gate(d, t, 3), func=ACT.Sigmoid)

        def fresh_part(n):
            d, t = units[n]
            fresh[n] = cell_pool.tile([P, HID], F32, name="fresh")
            nc.vector.tensor_tensor(out=fresh[n][:], in0=gate(d, t, 0), in1=gate(d, t, 2), op=ALU.mult)

        def new_cell(n):
            cell[n] = cell_pool.tile([P, HID], F32, name="cell")
            nc.vector.tensor_tensor(out=cell[n][:], in0=kept[n][:], in1=fresh[n][:], op=ALU.add)
            nc.scalar.activation(out=cell[n][:], in_=cell[n][:], func=ACT.Tanh)

        def new_hidden(n):
            d, t = units[n]
            hidden = cell_pool.tile([P, HID], F32, name="hidden")
            nc.vector.tensor_tensor(out=hidden[:], in0=gate(d, t, 3), in1=cell[n][:], op=ALU.mult)
            nc.sync.dma_start(out=out_view[:, t, d * HID:(d + 1) * HID], in_=hidden[:])

        stages = (activate_gates, fresh_part, new_cell, new_hidden)
        for n in range(len(units) + len(stages) - 1):
            for lag, stage_of in enumerate(stages):
                if 0 <= n - lag < len(units):
                    stage_of(n - lag)
